import numpy as np
import ml_dtypes

BF16 = ml_dtypes.bfloat16


def bf(x):
    return np.asarray(x, np.float32).astype(BF16)


def f32(x):
    return np.asarray(x, np.float32)


def f64(x):
    return np.asarray(x).astype(np.float64)


def striped(idx):
    return np.tile(idx.reshape(-1, 16).T, (8, 1))


H, S, N = 128, 1024, 768


def sigmoid(v):
    return 1.0 / (1.0 + np.exp(-v))


def setup_inputs():
    return {"base": f32(0.5 * np.random.standard_normal((H, S))), "x": bf(np.random.standard_normal((H, N))), "wz": bf(np.random.standard_normal((H, H)) / np.sqrt(H)), "bz": f32(0.2 * np.random.standard_normal((H, 1))), "wh": bf(np.random.standard_normal((H, H)) / np.sqrt(H)), "bh": f32(0.2 * np.random.standard_normal((H, 1))), "offs": striped(np.random.permutation(S)[:N])}


def reference(base, x, wz, bz, wh, bh, offs):
    idx = offs[:16].T.reshape(-1)
    z = sigmoid(f64(wz).T @ f64(x) + f64(bz))
    p = np.tanh(f64(wh).T @ f64(x) + f64(bh))
    out = f64(base).copy()
    out[:, idx] = z * p
    return out

@@ -1,0 +1,53 @@
+import concourse.mybir as mybir
+
+H = 128
+S = 1024
+N = 768
+HALF = N // 2
+
+FLOPS = 2 * 2 * H * H * N
+
+BF16, F32, U16 = mybir.dt.bfloat16, mybir.dt.float32, mybir.dt.uint16
+SIGMOID = mybir.ActivationFunctionType.Sigmoid
+TANH = mybir.ActivationFunctionType.Tanh
+MULT = mybir.AluOpType.mult
+
+
+def tile_generator_kernel(tc, base, x, wz, bz, wh, bh, offs, out):
+    nc = tc.nc
+    with (
+        tc.tile_pool(name="held", bufs=1) as held,
+        tc.psum_pool(name="psum", bufs=1) as psum,
+    ):
+        offsets = held.tile([H, N // 16], U16, name="offsets")
+        nc.sync.dma_start(offsets[:], offs)
+
+        x_sb = held.tile([H, N], BF16, name="x_sb")
+        nc.sync.dma_start(x_sb[:], x)
+        wz_sb = held.tile([H, H], BF16, name="wz_sb")
+        nc.scalar.dma_start(wz_sb[:], wz)
+        wh_sb = held.tile([H, H], BF16, name="wh_sb")
+        nc.scalar.dma_start(wh_sb[:], wh)
+        bz_sb = held.tile([H, 1], F32, name="bz_sb")
+        nc.gpsimd.dma_start(bz_sb[:], bz)
+        bh_sb = held.tile([H, 1], F32, name="bh_sb")
+        nc.gpsimd.dma_start(bh_sb[:], bh)
+
+        store = held.tile([H, S], F32, name="store")
+        nc.sync.dma_start(store[:], base)
+
+        z = held.tile([H, N], F32, name="z")
+        p = held.tile([H, N], F32, name="p")
+        for label, gate, w_sb, b_sb, func in (
+            ("z", z, wz_sb, bz_sb, SIGMOID),
+            ("p", p, wh_sb, bh_sb, TANH),
+        ):
+            for h in range(2):
+                cols = slice(h * HALF, (h + 1) * HALF)
+                acc = psum.tile([H, HALF], F32, name=f"acc_{label}{h}")
+                nc.tensor.matmul(acc[:], w_sb[:], x_sb[:, cols], start=True, stop=True)
+                nc.scalar.activation(gate[:, cols], acc[:], func, bias=b_sb[:])
+
+        nc.vector.tensor_tensor(store[:].indirect(offsets[:]), z[:], p[:], MULT)
+
+        nc.sync.dma_start(out, store[:])

@@ -29,9 +29,13 @@ def tile_generator_kernel(tc, base, x, wz, bz, wh, bh, offs, out):
         wh_sb = held.tile([H, H], BF16, name="wh_sb")
         nc.scalar.dma_start(wh_sb[:], wh)
         bz_sb = held.tile([H, 1], F32, name="bz_sb")
-        nc.gpsimd.dma_start(bz_sb[:], bz)
+        nc.scalar.dma_start(bz_sb[:], bz)
         bh_sb = held.tile([H, 1], F32, name="bh_sb")
-        nc.gpsimd.dma_start(bh_sb[:], bh)
+        nc.scalar.dma_start(bh_sb[:], bh)
+
+        warm = held.tile([H, 1], F32, name="warm")
+        nc.vector.memset(warm[:], 0.0)
+        nc.scalar.activation(warm[:], warm[:], SIGMOID)
 
         store = held.tile([H, S], F32, name="store")
         nc.sync.dma_start(store[:], base)

@@ -3,7 +3,8 @@ import concourse.mybir as mybir
 H = 128
 S = 1024
 N = 768
-HALF = N // 2
+PIECE = 256
+PIECES = N // PIECE
 
 FLOPS = 2 * 2 * H * H * N
 
@@ -17,7 +18,8 @@ def tile_generator_kernel(tc, base, x, wz, bz, wh, bh, offs, out):
     nc = tc.nc
     with (
         tc.tile_pool(name="held", bufs=1) as held,
-        tc.psum_pool(name="psum", bufs=1) as psum,
+        tc.tile_pool(name="gates", bufs=PIECES) as gates,
+        tc.psum_pool(name="psum", bufs=PIECES) as psum,
     ):
         offsets = held.tile([H, N // 16], U16, name="offsets")
         nc.sync.dma_start(offsets[:], offs)
@@ -40,18 +42,17 @@ def tile_generator_kernel(tc, base, x, wz, bz, wh, bh, offs, out):
         store = held.tile([H, S], F32, name="store")
         nc.sync.dma_start(store[:], base)
 
-        z = held.tile([H, N], F32, name="z")
-        p = held.tile([H, N], F32, name="p")
-        for label, gate, w_sb, b_sb, func in (
-            ("z", z, wz_sb, bz_sb, SIGMOID),
-            ("p", p, wh_sb, bh_sb, TANH),
-        ):
-            for h in range(2):
-                cols = slice(h * HALF, (h + 1) * HALF)
-                acc = psum.tile([H, HALF], F32, name=f"acc_{label}{h}")
-                nc.tensor.matmul(acc[:], w_sb[:], x_sb[:, cols], start=True, stop=True)
-                nc.scalar.activation(gate[:, cols], acc[:], func, bias=b_sb[:])
-
-        nc.vector.tensor_tensor(store[:].indirect(offsets[:]), z[:], p[:], MULT)
+        for i in range(PIECES):
+            cols = slice(i * PIECE, (i + 1) * PIECE)
+            acc_z = psum.tile([H, PIECE], F32, name="acc_z")
+            nc.tensor.matmul(acc_z[:], wz_sb[:], x_sb[:, cols], start=True, stop=True)
+            acc_p = psum.tile([H, PIECE], F32, name="acc_p")
+            nc.tensor.matmul(acc_p[:], wh_sb[:], x_sb[:, cols], start=True, stop=True)
+            z = gates.tile([H, PIECE], F32, name="z")
+            nc.scalar.activation(z[:], acc_z[:], SIGMOID, bias=bz_sb[:])
+            p = gates.tile([H, PIECE], F32, name="p")
+            nc.scalar.activation(p[:], acc_p[:], TANH, bias=bh_sb[:])
+            piece_offsets = offsets[:, i * (PIECE // 16) : (i + 1) * (PIECE // 16)]
+            nc.vector.tensor_tensor(store[:].indirect(piece_offsets), z[:], p[:], MULT)
 
         nc.sync.dma_start(out, store[:])

@@ -3,8 +3,8 @@ import concourse.mybir as mybir
 H = 128
 S = 1024
 N = 768
-PIECE = 256
-PIECES = N // PIECE
+WIDTHS = (256, 512)
+STARTS = (0, 256)
 
 FLOPS = 2 * 2 * H * H * N
 
@@ -18,41 +18,39 @@ def tile_generator_kernel(tc, base, x, wz, bz, wh, bh, offs, out):
     nc = tc.nc
     with (
         tc.tile_pool(name="held", bufs=1) as held,
-        tc.tile_pool(name="gates", bufs=PIECES) as gates,
-        tc.psum_pool(name="psum", bufs=PIECES) as psum,
+        tc.psum_pool(name="psum", bufs=1) as psum,
     ):
-        offsets = held.tile([H, N // 16], U16, name="offsets")
-        nc.sync.dma_start(offsets[:], offs)
-
-        x_sb = held.tile([H, N], BF16, name="x_sb")
-        nc.sync.dma_start(x_sb[:], x)
-        wz_sb = held.tile([H, H], BF16, name="wz_sb")
-        nc.scalar.dma_start(wz_sb[:], wz)
-        wh_sb = held.tile([H, H], BF16, name="wh_sb")
-        nc.scalar.dma_start(wh_sb[:], wh)
         bz_sb = held.tile([H, 1], F32, name="bz_sb")
-        nc.scalar.dma_start(bz_sb[:], bz)
         bh_sb = held.tile([H, 1], F32, name="bh_sb")
+        wz_sb = held.tile([H, H], BF16, name="wz_sb")
+        wh_sb = held.tile([H, H], BF16, name="wh_sb")
+        x_sb = [held.tile([H, width], BF16, name=f"x_sb{i}") for i, width in enumerate(WIDTHS)]
+        offsets = held.tile([H, N // 16], U16, name="offsets")
+        store = held.tile([H, S], F32, name="store")
+
+        nc.sync.dma_start(bz_sb[:], bz)
         nc.scalar.dma_start(bh_sb[:], bh)
+        nc.sync.dma_start(x_sb[0][:], x[:, STARTS[0] : STARTS[0] + WIDTHS[0]])
+        nc.scalar.dma_start(wz_sb[:], wz)
+        nc.scalar.dma_start(wh_sb[:], wh)
+        nc.sync.dma_start(offsets[:], offs)
+        nc.sync.dma_start(store[:], base)
+        nc.sync.dma_start(x_sb[1][:], x[:, STARTS[1] : STARTS[1] + WIDTHS[1]])
 
         warm = held.tile([H, 1], F32, name="warm")
         nc.vector.memset(warm[:], 0.0)
         nc.scalar.activation(warm[:], warm[:], SIGMOID)
 
-        store = held.tile([H, S], F32, name="store")
-        nc.sync.dma_start(store[:], base)
-
-        for i in range(PIECES):
-            cols = slice(i * PIECE, (i + 1) * PIECE)
-            acc_z = psum.tile([H, PIECE], F32, name="acc_z")
-            nc.tensor.matmul(acc_z[:], wz_sb[:], x_sb[:, cols], start=True, stop=True)
-            acc_p = psum.tile([H, PIECE], F32, name="acc_p")
-            nc.tensor.matmul(acc_p[:], wh_sb[:], x_sb[:, cols], start=True, stop=True)
-            z = gates.tile([H, PIECE], F32, name="z")
+        for i, (start, width) in enumerate(zip(STARTS, WIDTHS)):
+            acc_z = psum.tile([H, width], F32, name=f"acc_z{i}")
+            nc.tensor.matmul(acc_z[:], wz_sb[:], x_sb[i][:], start=True, stop=True)
+            acc_p = psum.tile([H, width], F32, name=f"acc_p{i}")
+            nc.tensor.matmul(acc_p[:], wh_sb[:], x_sb[i][:], start=True, stop=True)
+            z = held.tile([H, width], F32, name=f"z{i}")
             nc.scalar.activation(z[:], acc_z[:], SIGMOID, bias=bz_sb[:])
-            p = gates.tile([H, PIECE], F32, name="p")
+            p = held.tile([H, width], F32, name=f"p{i}")
             nc.scalar.activation(p[:], acc_p[:], TANH, bias=bh_sb[:])
-            piece_offsets = offsets[:, i * (PIECE // 16) : (i + 1) * (PIECE // 16)]
+            piece_offsets = offsets[:, start // 16 : (start + width) // 16]
             nc.vector.tensor_tensor(store[:].indirect(piece_offsets), z[:], p[:], MULT)
 
         nc.sync.dma_start(out, store[:])

@@ -28,13 +28,14 @@ def tile_generator_kernel(tc, base, x, wz, bz, wh, bh, offs, out):
         offsets = held.tile([H, N // 16], U16, name="offsets")
         store = held.tile([H, S], F32, name="store")
 
+        nc.sync.dma_start(store[0 : H // 2, :], base[0 : H // 2, :])
+        nc.scalar.dma_start(store[H // 2 : H, :], base[H // 2 : H, :])
         nc.sync.dma_start(bz_sb[:], bz)
         nc.scalar.dma_start(bh_sb[:], bh)
         nc.sync.dma_start(x_sb[0][:], x[:, STARTS[0] : STARTS[0] + WIDTHS[0]])
         nc.scalar.dma_start(wz_sb[:], wz)
         nc.scalar.dma_start(wh_sb[:], wh)
         nc.sync.dma_start(offsets[:], offs)
-        nc.sync.dma_start(store[:], base)
         nc.sync.dma_start(x_sb[1][:], x[:, STARTS[1] : STARTS[1] + WIDTHS[1]])
 
         warm = held.tile([H, 1], F32, name="warm")

@@ -3,8 +3,8 @@ import concourse.mybir as mybir
 H = 128
 S = 1024
 N = 768
-WIDTHS = (256, 512)
-STARTS = (0, 256)
+PIECE = 384
+PIECES = N // PIECE
 
 FLOPS = 2 * 2 * H * H * N
 
@@ -18,40 +18,40 @@ def tile_generator_kernel(tc, base, x, wz, bz, wh, bh, offs, out):
     nc = tc.nc
     with (
         tc.tile_pool(name="held", bufs=1) as held,
-        tc.psum_pool(name="psum", bufs=1) as psum,
+        tc.tile_pool(name="gates", bufs=PIECES) as gates,
+        tc.psum_pool(name="psum", bufs=PIECES) as psum,
     ):
         bz_sb = held.tile([H, 1], F32, name="bz_sb")
         bh_sb = held.tile([H, 1], F32, name="bh_sb")
         wz_sb = held.tile([H, H], BF16, name="wz_sb")
         wh_sb = held.tile([H, H], BF16, name="wh_sb")
-        x_sb = [held.tile([H, width], BF16, name=f"x_sb{i}") for i, width in enumerate(WIDTHS)]
+        x_sb = held.tile([H, N], BF16, name="x_sb")
         offsets = held.tile([H, N // 16], U16, name="offsets")
         store = held.tile([H, S], F32, name="store")
 
-        nc.sync.dma_start(store[0 : H // 2, :], base[0 : H // 2, :])
-        nc.scalar.dma_start(store[H // 2 : H, :], base[H // 2 : H, :])
         nc.sync.dma_start(bz_sb[:], bz)
         nc.scalar.dma_start(bh_sb[:], bh)
-        nc.sync.dma_start(x_sb[0][:], x[:, STARTS[0] : STARTS[0] + WIDTHS[0]])
+        nc.sync.dma_start(x_sb[:], x)
         nc.scalar.dma_start(wz_sb[:], wz)
         nc.scalar.dma_start(wh_sb[:], wh)
         nc.sync.dma_start(offsets[:], offs)
-        nc.sync.dma_start(x_sb[1][:], x[:, STARTS[1] : STARTS[1] + WIDTHS[1]])
+        nc.sync.dma_start(store[:], base)
 
         warm = held.tile([H, 1], F32, name="warm")
         nc.vector.memset(warm[:], 0.0)
         nc.scalar.activation(warm[:], warm[:], SIGMOID)
 
-        for i, (start, width) in enumerate(zip(STARTS, WIDTHS)):
-            acc_z = psum.tile([H, width], F32, name=f"acc_z{i}")
-            nc.tensor.matmul(acc_z[:], wz_sb[:], x_sb[i][:], start=True, stop=True)
-            acc_p = psum.tile([H, width], F32, name=f"acc_p{i}")
-            nc.tensor.matmul(acc_p[:], wh_sb[:], x_sb[i][:], start=True, stop=True)
-            z = held.tile([H, width], F32, name=f"z{i}")
+        for i in range(PIECES):
+            cols = slice(i * PIECE, (i + 1) * PIECE)
+            acc_z = psum.tile([H, PIECE], F32, name="acc_z")
+            nc.tensor.matmul(acc_z[:], wz_sb[:], x_sb[:, cols], start=True, stop=True)
+            acc_p = psum.tile([H, PIECE], F32, name="acc_p")
+            nc.tensor.matmul(acc_p[:], wh_sb[:], x_sb[:, cols], start=True, stop=True)
+            z = gates.tile([H, PIECE], F32, name="z")
             nc.scalar.activation(z[:], acc_z[:], SIGMOID, bias=bz_sb[:])
-            p = held.tile([H, width], F32, name=f"p{i}")
+            p = gates.tile([H, PIECE], F32, name="p")
             nc.scalar.activation(p[:], acc_p[:], TANH, bias=bh_sb[:])
-            piece_offsets = offsets[:, start // 16 : (start + width) // 16]
+            piece_offsets = offsets[:, i * (PIECE // 16) : (i + 1) * (PIECE // 16)]
             nc.vector.tensor_tensor(store[:].indirect(piece_offsets), z[:], p[:], MULT)
 
         nc.sync.dma_start(out, store[:])

@@ -5,6 +5,8 @@ S = 1024
 N = 768
 PIECE = 384
 PIECES = N // PIECE
+BLOCKS = 4
+BLOCK = S // BLOCKS
 
 FLOPS = 2 * 2 * H * H * N
 
@@ -35,7 +37,10 @@ def tile_generator_kernel(tc, base, x, wz, bz, wh, bh, offs, out):
         nc.scalar.dma_start(wz_sb[:], wz)
         nc.scalar.dma_start(wh_sb[:], wh)
         nc.sync.dma_start(offsets[:], offs)
-        nc.sync.dma_start(store[:], base)
+        for b in range(BLOCKS):
+            queue = nc.sync if b % 2 == 0 else nc.scalar
+            block = slice(b * BLOCK, (b + 1) * BLOCK)
+            queue.dma_start(store[:, block], base[:, block])
 
         warm = held.tile([H, 1], F32, name="warm")
         nc.vector.memset(warm[:], 0.0)
@@ -54,4 +59,7 @@ def tile_generator_kernel(tc, base, x, wz, bz, wh, bh, offs, out):
             piece_offsets = offsets[:, i * (PIECE // 16) : (i + 1) * (PIECE // 16)]
             nc.vector.tensor_tensor(store[:].indirect(piece_offsets), z[:], p[:], MULT)
 
-        nc.sync.dma_start(out, store[:])
+        for b in range(BLOCKS):
+            queue = nc.sync if b % 2 == 0 else nc.scalar
+            block = slice(b * BLOCK, (b + 1) * BLOCK)
+            queue.dma_start(out[:, block], store[:, block])

@@ -3,10 +3,7 @@ import concourse.mybir as mybir
 H = 128
 S = 1024
 N = 768
-PIECE = 384
-PIECES = N // PIECE
-BLOCKS = 4
-BLOCK = S // BLOCKS
+HALF = N // 2
 
 FLOPS = 2 * 2 * H * H * N
 
@@ -20,8 +17,7 @@ def tile_generator_kernel(tc, base, x, wz, bz, wh, bh, offs, out):
     nc = tc.nc
     with (
         tc.tile_pool(name="held", bufs=1) as held,
-        tc.tile_pool(name="gates", bufs=PIECES) as gates,
-        tc.psum_pool(name="psum", bufs=PIECES) as psum,
+        tc.psum_pool(name="psum", bufs=1) as psum,
     ):
         bz_sb = held.tile([H, 1], F32, name="bz_sb")
         bh_sb = held.tile([H, 1], F32, name="bh_sb")
@@ -31,35 +27,30 @@ def tile_generator_kernel(tc, base, x, wz, bz, wh, bh, offs, out):
         offsets = held.tile([H, N // 16], U16, name="offsets")
         store = held.tile([H, S], F32, name="store")
 
-        nc.sync.dma_start(bz_sb[:], bz)
-        nc.scalar.dma_start(bh_sb[:], bh)
         nc.sync.dma_start(x_sb[:], x)
         nc.scalar.dma_start(wz_sb[:], wz)
+        nc.sync.dma_start(bz_sb[:], bz)
         nc.scalar.dma_start(wh_sb[:], wh)
+        nc.scalar.dma_start(bh_sb[:], bh)
+        nc.sync.dma_start(store[:], base)
         nc.sync.dma_start(offsets[:], offs)
-        for b in range(BLOCKS):
-            queue = nc.sync if b % 2 == 0 else nc.scalar
-            block = slice(b * BLOCK, (b + 1) * BLOCK)
-            queue.dma_start(store[:, block], base[:, block])
 
         warm = held.tile([H, 1], F32, name="warm")
         nc.vector.memset(warm[:], 0.0)
         nc.scalar.activation(warm[:], warm[:], SIGMOID)
 
-        for i in range(PIECES):
-            cols = slice(i * PIECE, (i + 1) * PIECE)
-            acc_z = psum.tile([H, PIECE], F32, name="acc_z")
-            nc.tensor.matmul(acc_z[:], wz_sb[:], x_sb[:, cols], start=True, stop=True)
-            acc_p = psum.tile([H, PIECE], F32, name="acc_p")
-            nc.tensor.matmul(acc_p[:], wh_sb[:], x_sb[:, cols], start=True, stop=True)
-            z = gates.tile([H, PIECE], F32, name="z")
-            nc.scalar.activation(z[:], acc_z[:], SIGMOID, bias=bz_sb[:])
-            p = gates.tile([H, PIECE], F32, name="p")
-            nc.scalar.activation(p[:], acc_p[:], TANH, bias=bh_sb[:])
-            piece_offsets = offsets[:, i * (PIECE // 16) : (i + 1) * (PIECE // 16)]
-            nc.vector.tensor_tensor(store[:].indirect(piece_offsets), z[:], p[:], MULT)
+        z = held.tile([H, N], F32, name="z")
+        p = held.tile([H, N], F32, name="p")
+        for label, gate, w_sb, b_sb, func in (
+            ("z", z, wz_sb, bz_sb, SIGMOID),
+            ("p", p, wh_sb, bh_sb, TANH),
+        ):
+            for h in range(2):
+                cols = slice(h * HALF, (h + 1) * HALF)
+                acc = psum.tile([H, HALF], F32, name=f"acc_{label}{h}")
+                nc.tensor.matmul(acc[:], w_sb[:], x_sb[:, cols], start=True, stop=True)
+                nc.scalar.activation(gate[:, cols], acc[:], func, bias=b_sb[:])
 
-        for b in range(BLOCKS):
-            queue = nc.sync if b % 2 == 0 else nc.scalar
-            block = slice(b * BLOCK, (b + 1) * BLOCK)
-            queue.dma_start(out[:, block], store[:, block])
+        nc.vector.tensor_tensor(store[:].indirect(offsets[:]), z[:], p[:], MULT)
+
+        nc.sync.dma_start(out, store[:])

@@ -3,7 +3,7 @@ import concourse.mybir as mybir
 H = 128
 S = 1024
 N = 768
-HALF = N // 2
+PIECE = 384
 
 FLOPS = 2 * 2 * H * H * N
 
@@ -39,18 +39,17 @@ def tile_generator_kernel(tc, base, x, wz, bz, wh, bh, offs, out):
         nc.vector.memset(warm[:], 0.0)
         nc.scalar.activation(warm[:], warm[:], SIGMOID)
 
-        z = held.tile([H, N], F32, name="z")
-        p = held.tile([H, N], F32, name="p")
-        for label, gate, w_sb, b_sb, func in (
-            ("z", z, wz_sb, bz_sb, SIGMOID),
-            ("p", p, wh_sb, bh_sb, TANH),
-        ):
-            for h in range(2):
-                cols = slice(h * HALF, (h + 1) * HALF)
-                acc = psum.tile([H, HALF], F32, name=f"acc_{label}{h}")
-                nc.tensor.matmul(acc[:], w_sb[:], x_sb[:, cols], start=True, stop=True)
-                nc.scalar.activation(gate[:, cols], acc[:], func, bias=b_sb[:])
-
-        nc.vector.tensor_tensor(store[:].indirect(offsets[:]), z[:], p[:], MULT)
+        for i in range(N // PIECE):
+            cols = slice(i * PIECE, (i + 1) * PIECE)
+            acc_z = psum.tile([H, PIECE], F32, name=f"acc_z{i}")
+            acc_p = psum.tile([H, PIECE], F32, name=f"acc_p{i}")
+            z = held.tile([H, PIECE], F32, name=f"z{i}")
+            p = held.tile([H, PIECE], F32, name=f"p{i}")
+            nc.tensor.matmul(acc_z[:], wz_sb[:], x_sb[:, cols], start=True, stop=True)
+            nc.tensor.matmul(acc_p[:], wh_sb[:], x_sb[:, cols], start=True, stop=True)
+            nc.scalar.activation(z[:], acc_z[:], SIGMOID, bias=bz_sb[:])
+            nc.scalar.activation(p[:], acc_p[:], TANH, bias=bh_sb[:])
+            piece_offsets = offsets[:, i * PIECE // 16 : (i + 1) * PIECE // 16]
+            nc.vector.tensor_tensor(store[:].indirect(piece_offsets), z[:], p[:], MULT)
 
         nc.sync.dma_start(out, store[:])

@@ -36,13 +36,13 @@ def tile_generator_kernel(tc, base, x, wz, bz, wh, bh, offs, out):
         nc.sync.dma_start(offsets[:], offs)
 
         warm = held.tile([H, 1], F32, name="warm")
-        nc.vector.memset(warm[:], 0.0)
+        nc.gpsimd.memset(warm[:], 0.0)
         nc.scalar.activation(warm[:], warm[:], SIGMOID)
 
         for i in range(N // PIECE):
             cols = slice(i * PIECE, (i + 1) * PIECE)
-            acc_z = psum.tile([H, PIECE], F32, name=f"acc_z{i}")
-            acc_p = psum.tile([H, PIECE], F32, name=f"acc_p{i}")
+            acc_z = psum.tile([H, PIECE], F32, name="acc_z")
+            acc_p = psum.tile([H, PIECE], F32, name="acc_p")
             z = held.tile([H, PIECE], F32, name=f"z{i}")
             p = held.tile([H, PIECE], F32, name=f"p{i}")
             nc.tensor.matmul(acc_z[:], wz_sb[:], x_sb[:, cols], start=True, stop=True)

@@ -3,6 +3,7 @@ import concourse.mybir as mybir
 H = 128
 S = 1024
 N = 768
+BLOCK = 32
 PIECE = 384
 
 FLOPS = 2 * 2 * H * H * N
@@ -19,21 +20,26 @@ def tile_generator_kernel(tc, base, x, wz, bz, wh, bh, offs, out):
         tc.tile_pool(name="held", bufs=1) as held,
         tc.psum_pool(name="psum", bufs=1) as psum,
     ):
-        bz_sb = held.tile([H, 1], F32, name="bz_sb")
-        bh_sb = held.tile([H, 1], F32, name="bh_sb")
+        bias_rows = held.tile([H, 2 * BLOCK], F32, name="bias_rows", align_bytes=64)
+        bias_cols = held.tile([H, 2 * BLOCK], F32, name="bias_cols", align_bytes=64)
         wz_sb = held.tile([H, H], BF16, name="wz_sb")
         wh_sb = held.tile([H, H], BF16, name="wh_sb")
         x_sb = held.tile([H, N], BF16, name="x_sb")
         offsets = held.tile([H, N // 16], U16, name="offsets")
         store = held.tile([H, S], F32, name="store")
 
+        nc.gpsimd.memset(bias_rows[:], 0.0)
         nc.sync.dma_start(x_sb[:], x)
         nc.scalar.dma_start(wz_sb[:], wz)
-        nc.sync.dma_start(bz_sb[:], bz)
+        nc.sync.dma_start(bias_rows[0:H:BLOCK, 0:BLOCK], bz.rearrange("(q i) o -> q (i o)", i=BLOCK))
         nc.scalar.dma_start(wh_sb[:], wh)
-        nc.scalar.dma_start(bh_sb[:], bh)
+        nc.sync.dma_start(bias_rows[0:H:BLOCK, BLOCK : 2 * BLOCK], bh.rearrange("(q i) o -> q (i o)", i=BLOCK))
         nc.sync.dma_start(store[:], base)
         nc.sync.dma_start(offsets[:], offs)
+
+        nc.vector.transpose(bias_cols[:, 0:BLOCK], bias_rows[:, 0:BLOCK])
+        nc.vector.transpose(bias_cols[:, BLOCK : 2 * BLOCK], bias_rows[:, BLOCK : 2 * BLOCK])
+        bz_sb, bh_sb = bias_cols[:, 0:1], bias_cols[:, BLOCK : BLOCK + 1]
 
         warm = held.tile([H, 1], F32, name="warm")
         nc.gpsimd.memset(warm[:], 0.0)
@@ -47,8 +53,8 @@ def tile_generator_kernel(tc, base, x, wz, bz, wh, bh, offs, out):
             p = held.tile([H, PIECE], F32, name=f"p{i}")
             nc.tensor.matmul(acc_z[:], wz_sb[:], x_sb[:, cols], start=True, stop=True)
             nc.tensor.matmul(acc_p[:], wh_sb[:], x_sb[:, cols], start=True, stop=True)
-            nc.scalar.activation(z[:], acc_z[:], SIGMOID, bias=bz_sb[:])
-            nc.scalar.activation(p[:], acc_p[:], TANH, bias=bh_sb[:])
+            nc.scalar.activation(z[:], acc_z[:], SIGMOID, bias=bz_sb)
+            nc.scalar.activation(p[:], acc_p[:], TANH, bias=bh_sb)
             piece_offsets = offsets[:, i * PIECE // 16 : (i + 1) * PIECE // 16]
             nc.vector.tensor_tensor(store[:].indirect(piece_offsets), z[:], p[:], MULT)
 

@@ -4,7 +4,9 @@ H = 128
 S = 1024
 N = 768
 BLOCK = 32
-PIECE = 384
+BANK = 512
+PIECES = (256, 512)
+assert sum(PIECES) == N and max(PIECES) <= BANK
 
 FLOPS = 2 * 2 * H * H * N
 
@@ -45,17 +47,19 @@ def tile_generator_kernel(tc, base, x, wz, bz, wh, bh, offs, out):
         nc.gpsimd.memset(warm[:], 0.0)
         nc.scalar.activation(warm[:], warm[:], SIGMOID)
 
-        for i in range(N // PIECE):
-            cols = slice(i * PIECE, (i + 1) * PIECE)
-            acc_z = psum.tile([H, PIECE], F32, name="acc_z")
-            acc_p = psum.tile([H, PIECE], F32, name="acc_p")
-            z = held.tile([H, PIECE], F32, name=f"z{i}")
-            p = held.tile([H, PIECE], F32, name=f"p{i}")
-            nc.tensor.matmul(acc_z[:], wz_sb[:], x_sb[:, cols], start=True, stop=True)
-            nc.tensor.matmul(acc_p[:], wh_sb[:], x_sb[:, cols], start=True, stop=True)
-            nc.scalar.activation(z[:], acc_z[:], SIGMOID, bias=bz_sb)
-            nc.scalar.activation(p[:], acc_p[:], TANH, bias=bh_sb)
-            piece_offsets = offsets[:, i * PIECE // 16 : (i + 1) * PIECE // 16]
+        first = 0
+        for i, n in enumerate(PIECES):
+            cols = slice(first, first + n)
+            acc_z = psum.tile([H, BANK], F32, name="acc_z")
+            acc_p = psum.tile([H, BANK], F32, name="acc_p")
+            z = held.tile([H, n], F32, name=f"z{i}")
+            p = held.tile([H, n], F32, name=f"p{i}")
+            nc.tensor.matmul(acc_z[:, 0:n], wz_sb[:], x_sb[:, cols], start=True, stop=True)
+            nc.tensor.matmul(acc_p[:, 0:n], wh_sb[:], x_sb[:, cols], start=True, stop=True)
+            nc.scalar.activation(z[:], acc_z[:, 0:n], SIGMOID, bias=bz_sb)
+            nc.scalar.activation(p[:], acc_p[:, 0:n], TANH, bias=bh_sb)
+            piece_offsets = offsets[:, first // 16 : (first + n) // 16]
             nc.vector.tensor_tensor(store[:].indirect(piece_offsets), z[:], p[:], MULT)
+            first += n
 
         nc.sync.dma_start(out, store[:])

@@ -36,8 +36,8 @@ def tile_generator_kernel(tc, base, x, wz, bz, wh, bh, offs, out):
         nc.sync.dma_start(bias_rows[0:H:BLOCK, 0:BLOCK], bz.rearrange("(q i) o -> q (i o)", i=BLOCK))
         nc.scalar.dma_start(wh_sb[:], wh)
         nc.sync.dma_start(bias_rows[0:H:BLOCK, BLOCK : 2 * BLOCK], bh.rearrange("(q i) o -> q (i o)", i=BLOCK))
-        nc.sync.dma_start(store[:], base)
         nc.sync.dma_start(offsets[:], offs)
+        nc.sync.dma_start(store[:], base)
 
         nc.vector.transpose(bias_cols[:, 0:BLOCK], bias_rows[:, 0:BLOCK])
         nc.vector.transpose(bias_cols[:, BLOCK : 2 * BLOCK], bias_rows[:, BLOCK : 2 * BLOCK])

@@ -20,33 +20,34 @@ def tile_generator_kernel(tc, base, x, wz, bz, wh, bh, offs, out):
     nc = tc.nc
     with (
         tc.tile_pool(name="held", bufs=1) as held,
-        tc.psum_pool(name="psum", bufs=1) as psum,
+        tc.psum_pool(name="psum", bufs=2) as psum,
     ):
-        bias_rows = held.tile([H, 2 * BLOCK], F32, name="bias_rows", align_bytes=64)
-        bias_cols = held.tile([H, 2 * BLOCK], F32, name="bias_cols", align_bytes=64)
-        wz_sb = held.tile([H, H], BF16, name="wz_sb")
-        wh_sb = held.tile([H, H], BF16, name="wh_sb")
+        bias_rows = held.tile([H, BLOCK], F32, name="bias_rows", align_bytes=64)
+        bias_cols = held.tile([H, BLOCK], F32, name="bias_cols", align_bytes=64)
+        weights = held.tile([H, 2 * H], BF16, name="weights")
+        weights_copy = held.tile([H, 2 * H], BF16, name="weights_copy")
         x_sb = held.tile([H, N], BF16, name="x_sb")
         offsets = held.tile([H, N // 16], U16, name="offsets")
         store = held.tile([H, S], F32, name="store")
 
         nc.gpsimd.memset(bias_rows[:], 0.0)
         nc.sync.dma_start(x_sb[:], x)
-        nc.scalar.dma_start(wz_sb[:], wz)
-        nc.sync.dma_start(bias_rows[0:H:BLOCK, 0:BLOCK], bz.rearrange("(q i) o -> q (i o)", i=BLOCK))
-        nc.scalar.dma_start(wh_sb[:], wh)
-        nc.sync.dma_start(bias_rows[0:H:BLOCK, BLOCK : 2 * BLOCK], bh.rearrange("(q i) o -> q (i o)", i=BLOCK))
+        nc.scalar.dma_start(weights[:, 0:H], wz)
+        nc.sync.dma_start(bias_rows[0:H:BLOCK, :], bz.rearrange("(q i) o -> q (i o)", i=BLOCK))
+        nc.scalar.dma_start(weights[:, H : 2 * H], wh)
+        nc.sync.dma_start(bias_rows[1:H:BLOCK, :], bh.rearrange("(q i) o -> q (i o)", i=BLOCK))
         nc.sync.dma_start(offsets[:], offs)
         nc.sync.dma_start(store[:], base)
 
-        nc.vector.transpose(bias_cols[:, 0:BLOCK], bias_rows[:, 0:BLOCK])
-        nc.vector.transpose(bias_cols[:, BLOCK : 2 * BLOCK], bias_rows[:, BLOCK : 2 * BLOCK])
-        bz_sb, bh_sb = bias_cols[:, 0:1], bias_cols[:, BLOCK : BLOCK + 1]
+        nc.vector.transpose(bias_cols[:], bias_rows[:])
+        bz_sb, bh_sb = bias_cols[:, 0:1], bias_cols[:, 1:2]
 
         warm = held.tile([H, 1], F32, name="warm")
         nc.gpsimd.memset(warm[:], 0.0)
         nc.scalar.activation(warm[:], warm[:], SIGMOID)
 
+        nc.gpsimd.tensor_copy(weights_copy[:], weights[:])
+        weights_of_piece = (weights, weights_copy)
         first = 0
         for i, n in enumerate(PIECES):
             cols = slice(first, first + n)
@@ -54,8 +55,8 @@ def tile_generator_kernel(tc, base, x, wz, bz, wh, bh, offs, out):
             acc_p = psum.tile([H, BANK], F32, name="acc_p")
             z = held.tile([H, n], F32, name=f"z{i}")
             p = held.tile([H, n], F32, name=f"p{i}")
-            nc.tensor.matmul(acc_z[:, 0:n], wz_sb[:], x_sb[:, cols], start=True, stop=True)
-            nc.tensor.matmul(acc_p[:, 0:n], wh_sb[:], x_sb[:, cols], start=True, stop=True)
+            nc.tensor.matmul(acc_z[:, 0:n], weights_of_piece[i][:, 0:H], x_sb[:, cols], start=True, stop=True)
+            nc.tensor.matmul(acc_p[:, 0:n], weights_of_piece[i][:, H : 2 * H], x_sb[:, cols], start=True, stop=True)
             nc.scalar.activation(z[:], acc_z[:, 0:n], SIGMOID, bias=bz_sb)
             nc.scalar.activation(p[:], acc_p[:, 0:n], TANH, bias=bh_sb)
             piece_offsets = offsets[:, first // 16 : (first + n) // 16]

import concourse.mybir as mybir

H = 128
S = 1024
N = 768
BLOCK = 32
BANK = 512
PIECES = (256, 512)
assert sum(PIECES) == N and max(PIECES) <= BANK

FLOPS = 2 * 2 * H * H * N

BF16, F32, U16 = mybir.dt.bfloat16, mybir.dt.float32, mybir.dt.uint16
SIGMOID = mybir.ActivationFunctionType.Sigmoid
TANH = mybir.ActivationFunctionType.Tanh
MULT = mybir.AluOpType.mult


def tile_generator_kernel(tc, base, x, wz, bz, wh, bh, offs, out):
    nc = tc.nc
    with (
        tc.tile_pool(name="held", bufs=1) as held,
        tc.psum_pool(name="psum", bufs=2) as psum,
    ):
        bias_rows = held.tile([H, BLOCK], F32, name="bias_rows", align_bytes=64)
        bias_cols = held.tile([H, BLOCK], F32, name="bias_cols", align_bytes=64)
        weights = held.tile([H, 2 * H], BF16, name="weights")
        weights_copy = held.tile([H, 2 * H], BF16, name="weights_copy")
        x_sb = held.tile([H, N], BF16, name="x_sb")
        offsets = held.tile([H, N // 16], U16, name="offsets")
        store = held.tile([H, S], F32, name="store")

        nc.gpsimd.memset(bias_rows[:], 0.0)
        nc.sync.dma_start(x_sb[:], x)
        nc.scalar.dma_start(weights[:, 0:H], wz)
        nc.sync.dma_start(bias_rows[0:H:BLOCK, :], bz.rearrange("(q i) o -> q (i o)", i=BLOCK))
        nc.scalar.dma_start(weights[:, H : 2 * H], wh)
        nc.sync.dma_start(bias_rows[1:H:BLOCK, :], bh.rearrange("(q i) o -> q (i o)", i=BLOCK))
        nc.sync.dma_start(offsets[:], offs)
        nc.sync.dma_start(store[:], base)

        nc.vector.transpose(bias_cols[:], bias_rows[:])
        bz_sb, bh_sb = bias_cols[:, 0:1], bias_cols[:, 1:2]

        warm = held.tile([H, 1], F32, name="warm")
        nc.gpsimd.memset(warm[:], 0.0)
        nc.scalar.activation(warm[:], warm[:], SIGMOID)

        nc.gpsimd.tensor_copy(weights_copy[:], weights[:])
        weights_of_piece = (weights, weights_copy)
        first = 0
        for i, n in enumerate(PIECES):
            cols = slice(first, first + n)
            acc_z = psum.tile([H, BANK], F32, name="acc_z")
            acc_p = psum.tile([H, BANK], F32, name="acc_p")
            z = held.tile([H, n], F32, name=f"z{i}")
            p = held.tile([H, n], F32, name=f"p{i}")
            nc.tensor.matmul(acc_z[:, 0:n], weights_of_piece[i][:, 0:H], x_sb[:, cols], start=True, stop=True)
            nc.tensor.matmul(acc_p[:, 0:n], weights_of_piece[i][:, H : 2 * H], x_sb[:, cols], start=True, stop=True)
            nc.scalar.activation(z[:], acc_z[:, 0:n], SIGMOID, bias=bz_sb)
            nc.scalar.activation(p[:], acc_p[:, 0:n], TANH, bias=bh_sb)
            piece_offsets = offsets[:, first // 16 : (first + n) // 16]
            nc.vector.tensor_tensor(store[:].indirect(piece_offsets), z[:], p[:], MULT)
            first += n

        nc.sync.dma_start(out, store[:])
